import numpy as np
import ml_dtypes


def mxq(x, axis, fmt="e4m3"):
    dtype, down = {"e4m3": (ml_dtypes.float8_e4m3fn, 7), "e5m2": (ml_dtypes.float8_e5m2, 14)}[fmt]
    v = np.moveaxis(np.asarray(x, np.float32).astype(ml_dtypes.bfloat16).astype(np.float64), axis, -1)
    blocks = v.reshape(v.shape[:-1] + (-1, 32))
    amax = np.abs(blocks).max(-1, keepdims=True)
    byte = np.maximum(np.where(amax > 0, np.frexp(amax)[1] - 1 + 127, 0) - down, 1)
    scale = np.exp2(byte - 127.0)
    codes = (blocks / scale).astype(np.float32).astype(dtype).astype(np.float64)
    return np.moveaxis((codes * scale).reshape(v.shape), -1, axis)


WIDE = False


def mx_kscale(k):
    if not WIDE:
        return np.ones(k)
    levels = np.array([10, -10, 5, -5, 0])
    a = np.random.permutation(np.resize(levels, k // 512 * 4)).reshape(k // 512, 4)
    idx = np.arange(k)
    return np.exp2(a[idx // 512, idx % 128 // 32])


BF16 = ml_dtypes.bfloat16


def bf(x):
    return np.asarray(x, np.float32).astype(BF16)


def f64(x):
    return np.asarray(x).astype(np.float64)


E2M1 = np.array([0.0, 0.5, 1.0, 1.5, 2.0, 3.0, 4.0, 6.0, -0.0, -0.5, -1.0, -1.5, -2.0, -3.0, -4.0, -6.0])


def pack_weight(w, fmt):
    k, n = w.shape
    w = f64(bf(w)).reshape(k // 32, 32, n)
    amax = np.abs(w).max(1)
    if fmt == "e4m3":
        byte = np.frexp(amax)[1] - 1 + 127 - 7
    else:
        mant, ex = np.frexp(amax / 6.0)
        byte = np.where(mant > 0.5, ex, ex - 1) + 127
    byte = np.clip(np.where(amax > 0, byte, 1), 1, 254)
    scaled = (w * np.exp2(127.0 - byte)[:, None, :]).reshape(k, n).astype(np.float32)
    by_word = np.ascontiguousarray(scaled.reshape(k // 512, 128, 4, n).transpose(0, 1, 3, 2))
    if fmt == "e4m3":
        words = by_word.astype(ml_dtypes.float8_e4m3fn).view(np.uint8)
    else:
        c = by_word.astype(ml_dtypes.float4_e2m1fn).view(np.uint8) & 0xF
        words = c[..., 0::2] | (c[..., 1::2] << 4)
    return np.ascontiguousarray(words), np.ascontiguousarray(byte.astype(np.uint8).reshape(k // 512, 16, n))


def unpack_weight(words, scales, fmt):
    g, p, n, _ = words.shape
    if fmt == "e4m3":
        vals = np.ascontiguousarray(words).view(ml_dtypes.float8_e4m3fn).astype(np.float64)
    else:
        nib = np.empty((g, p, n, 4), np.uint8)
        nib[..., 0::2] = words & 0xF
        nib[..., 1::2] = words >> 4
        vals = E2M1[nib]
    vals = vals * np.repeat(np.exp2(scales.astype(np.float64) - 127.0), 8, axis=1)[..., None]
    return vals.transpose(0, 1, 3, 2).reshape(g * 512, n)


B, C, H, L = 1, 15872, 512, 128


def sigmoid(v):
    return 1.0 / (1.0 + np.exp(-v))


def pconv(xq, W_words, W_scales, b):
    return (unpack_weight(W_words, W_scales, "e4m3").T @ xq) + f64(b)[None, :, None]


def setup_inputs():
    s = np.concatenate([mx_kscale(C + H)[:C], np.ones(H)])
    w = lambda: pack_weight(np.ascontiguousarray((np.random.standard_normal((H, C + H)) / np.sqrt(C + H) / s).T), "e4m3")
    b = lambda: bf(np.random.standard_normal(H) * 0.3)
    inp = bf(np.random.standard_normal((B, C, L)) * s[:C, None])
    h = bf(np.random.standard_normal((B, H, L)))
    W_r_words, W_r_scales = w()
    b_r = b()
    W_u_words, W_u_scales = w()
    b_u = b()
    W_h_words, W_h_scales = w()
    b_h = b()
    return {"input": inp, "h": h,
            "W_r_words": W_r_words, "W_r_scales": W_r_scales, "b_r": b_r,
            "W_u_words": W_u_words, "W_u_scales": W_u_scales, "b_u": b_u,
            "W_h_words": W_h_words, "W_h_scales": W_h_scales, "b_h": b_h}


def reference(input, h, W_r_words, W_r_scales, b_r, W_u_words, W_u_scales, b_u, W_h_words, W_h_scales, b_h):
    h = f64(h)
    xq = mxq(f64(input), 1, "e4m3")
    input_h = np.concatenate([xq, mxq(h, 1, "e4m3")], axis=1)
    reset_h = sigmoid(pconv(input_h, W_r_words, W_r_scales, b_r))
    update_h = sigmoid(pconv(input_h, W_u_words, W_u_scales, b_u))
    input_new_h = np.concatenate([xq, mxq(h * reset_h, 1, "e4m3")], axis=1)
    new_h = np.tanh(pconv(input_new_h, W_h_words, W_h_scales, b_h))
    return (1.0 - update_h) * new_h + update_h * h

@@ -1,0 +1,175 @@
+from contextlib import ExitStack
+
+import concourse.mybir as mybir
+from concourse.masks import make_identity
+
+F32 = mybir.dt.float32
+BF16 = mybir.dt.bfloat16
+I32 = mybir.dt.int32
+U32 = mybir.dt.uint32
+U8 = mybir.dt.uint8
+FP8X4 = mybir.dt.float8_e4m3fn_x4
+ACT = mybir.ActivationFunctionType
+ALU = mybir.AluOpType
+
+P = 128
+PACK = 4
+L = 128
+H = 512
+X_GROUPS = 31
+GROUPS = X_GROUPS + 1
+HR_SLOT = GROUPS
+CHUNK = 4
+CHUNKS = GROUPS // CHUNK
+M_TILES = H // P
+W_BUFS = 16
+
+FLOPS = 2 * 3 * GROUPS * P * PACK * H * L
+
+
+def load_scale_planes(nc, planes, scales):
+    by_offset = scales.bitcast(F32).rearrange("(c j) q n -> j q c n", j=CHUNK)
+    for quadrant in range(4):
+        for row in range(4):
+            nc.gpsimd.dma_start(
+                out=planes[32 * quadrant + row : 32 * quadrant + 4 * CHUNK : 4, :, :].bitcast(F32),
+                in_=by_offset[:, 4 * quadrant + row, :, :],
+            )
+
+
+def load_words(nc, pool, words, c):
+    w = pool.tile([P, CHUNK, H], I32, tag="w", align_bytes=64)
+    rows = words[CHUNK * c : CHUNK * (c + 1)].rearrange("g p n t -> p g (n t)")
+    nc.sync.dma_start(out=w[:], in_=rows.bitcast(I32))
+    return w
+
+
+def channel_major_passes(nc, acc, w, planes, c, codes, code_planes, last_slot):
+    for m in range(M_TILES):
+        cols = slice(P * m, P * (m + 1))
+        for j in range(CHUNK):
+            g = CHUNK * c + j
+            slot = g if g < GROUPS - 1 else last_slot
+            nc.tensor.matmul_mx(
+                out=acc[m][:],
+                lhsT=w[:, j, cols].bitcast(FP8X4),
+                lhsT_scale=planes[4 * j : P, c, cols],
+                rhs=codes[:, slot, :].bitcast(FP8X4),
+                rhs_scale=code_planes[:, slot, :],
+                start=(g == 0),
+                stop=(g == GROUPS - 1),
+            )
+
+
+def tile_gru_k_kernel(
+    tc, x, h, w_r_words, w_r_scales, b_r, w_u_words, w_u_scales, b_u, w_h_words, w_h_scales, b_h, out
+):
+    nc = tc.nc
+    with ExitStack() as ctx:
+        ctx.enter_context(tc.manual_schedule())
+        keep = ctx.enter_context(tc.tile_pool(name="keep", bufs=1))
+        stage = ctx.enter_context(tc.tile_pool(name="stage", bufs=3))
+        stream = ctx.enter_context(tc.tile_pool(name="stream", bufs=W_BUFS))
+        psum = ctx.enter_context(tc.psum_pool(name="psum", bufs=1))
+
+        planes_r = keep.tile([P, CHUNKS, H], U8, align_bytes=64)
+        planes_u = keep.tile([P, CHUNKS, H], U8, align_bytes=64)
+        planes_h = keep.tile([P, CHUNKS, H], U8, align_bytes=64)
+        identity = keep.tile([P, P], F32)
+        make_identity(nc, identity[:])
+        for planes, scales in ((planes_r, w_r_scales), (planes_u, w_u_scales), (planes_h, w_h_scales)):
+            nc.vector.memset(planes[:].bitcast(I32), 0)
+            load_scale_planes(nc, planes, scales)
+
+        h_by_k = keep.tile([P, PACK, L], BF16)
+        h_by_tile = keep.tile([P, M_TILES, L], BF16)
+        nc.scalar.dma_start(out=h_by_k[:], in_=h[0].rearrange("(p t) l -> p t l", t=PACK))
+        nc.scalar.dma_start(out=h_by_tile[:], in_=h[0].rearrange("(m p) l -> p m l", p=P))
+        bias_r = keep.tile([P, PACK], BF16)
+        bias_u = keep.tile([P, M_TILES], BF16)
+        bias_h = keep.tile([P, M_TILES], BF16)
+        with nc.allow_non_contiguous_dma(reason="three biases of 512 values, one value a piece"):
+            nc.scalar.dma_start(out=bias_r[:], in_=b_r.rearrange("(p t) -> p t", t=PACK))
+            nc.scalar.dma_start(out=bias_u[:], in_=b_u.rearrange("(m p) -> p m", p=P))
+            nc.scalar.dma_start(out=bias_h[:], in_=b_h.rearrange("(m p) -> p m", p=P))
+
+        codes = keep.tile([P, GROUPS + 1, L], U32, align_bytes=64)
+        code_planes = keep.tile([P, GROUPS + 1, L], U8, align_bytes=64)
+        x_by_k = x[0].rearrange("(g p t) l -> p g t l", p=P, t=PACK)
+
+        acc_r = psum.tile([P, H], F32, tag="bank0")
+        for c in range(CHUNKS):
+            x_groups = min(CHUNK, X_GROUPS - CHUNK * c)
+            raw = stage.tile([P, CHUNK, PACK, L], BF16)
+            nc.sync.dma_start(out=raw[:, :x_groups], in_=x_by_k[:, CHUNK * c : CHUNK * c + x_groups])
+            w = load_words(nc, stream, w_r_words, c)
+            grouped = stage.tile([P, CHUNK, L, PACK], BF16, align_bytes=64)
+            nc.vector.tensor_copy(
+                out=grouped[:, :x_groups], in_=raw[:, :x_groups].rearrange("p g t l -> p g l t")
+            )
+            if x_groups < CHUNK:
+                nc.vector.tensor_copy(out=grouped[:, CHUNK - 1], in_=h_by_k[:].rearrange("p t l -> p l t"))
+            slots = slice(CHUNK * c, CHUNK * (c + 1))
+            nc.vector.quantize_mx(
+                out=codes[:, slots, :].rearrange("p g l -> p (g l)").bitcast(FP8X4),
+                scales=code_planes[:, slots, :].rearrange("p g l -> p (g l)"),
+                in_=grouped[:].rearrange("p g l t -> p (g l t)"),
+            )
+            for j in range(CHUNK):
+                g = CHUNK * c + j
+                nc.tensor.matmul_mx(
+                    out=acc_r[:],
+                    lhsT=codes[:, g, :].bitcast(FP8X4),
+                    lhsT_scale=code_planes[:, g, :],
+                    rhs=w[:, j, :].bitcast(FP8X4),
+                    rhs_scale=planes_r[4 * j : P, c, :],
+                    start=(g == 0),
+                    stop=(g == GROUPS - 1),
+                )
+
+        r_pre_t = keep.tile([P, PACK, P], F32)
+        nc.vector.tensor_copy(out=r_pre_t[:], in_=acc_r[:].rearrange("l (p t) -> l t p", t=PACK))
+        r_pre = psum.tile([P, PACK, L], F32, tag="bank1")
+        for t in range(PACK):
+            nc.tensor.transpose(r_pre[:, t, :], r_pre_t[:, t, :], identity[:])
+        r = keep.tile([P, PACK, L], F32)
+        for t in range(PACK):
+            nc.scalar.activation(out=r[:, t, :], in_=r_pre[:, t, :], func=ACT.Sigmoid, bias=bias_r[:, t : t + 1])
+        hr_grouped = keep.tile([P, L, PACK], BF16, align_bytes=64)
+        nc.vector.tensor_tensor(
+            out=hr_grouped[:],
+            in0=h_by_k[:].rearrange("p t l -> p l t"),
+            in1=r[:].rearrange("p t l -> p l t"),
+            op=ALU.mult,
+        )
+        nc.vector.quantize_mx(
+            out=codes[:, HR_SLOT, :].bitcast(FP8X4),
+            scales=code_planes[:, HR_SLOT, :],
+            in_=hr_grouped[:].rearrange("p l t -> p (l t)"),
+        )
+
+        acc_u = [psum.tile([P, L], F32, name="acc_u%d" % m, tag="bank%d" % (4 + m)) for m in range(M_TILES)]
+        for c in range(CHUNKS):
+            w = load_words(nc, stream, w_u_words, c)
+            channel_major_passes(nc, acc_u, w, planes_u, c, codes, code_planes, GROUPS - 1)
+        u = keep.tile([P, M_TILES, L], F32)
+        for m in range(M_TILES):
+            nc.scalar.activation(out=u[:, m, :], in_=acc_u[m][:], func=ACT.Sigmoid, bias=bias_u[:, m : m + 1])
+        one_minus_u = keep.tile([P, M_TILES, L], F32)
+        nc.vector.tensor_scalar(
+            out=one_minus_u[:], in0=u[:], scalar1=-1.0, scalar2=1.0, op0=ALU.mult, op1=ALU.add
+        )
+        u_h = keep.tile([P, M_TILES, L], F32)
+        nc.vector.tensor_tensor(out=u_h[:], in0=u[:], in1=h_by_tile[:], op=ALU.mult)
+
+        acc_n = [psum.tile([P, L], F32, name="acc_n%d" % m, tag="bank%d" % m) for m in range(M_TILES)]
+        for c in range(CHUNKS):
+            w = load_words(nc, stream, w_h_words, c)
+            channel_major_passes(nc, acc_n, w, planes_h, c, codes, code_planes, HR_SLOT)
+        n = keep.tile([P, M_TILES, L], F32)
+        blend = keep.tile([P, M_TILES, L], F32)
+        for m in range(M_TILES):
+            nc.scalar.activation(out=n[:, m, :], in_=acc_n[m][:], func=ACT.Tanh, bias=bias_h[:, m : m + 1])
+            nc.vector.tensor_tensor(out=blend[:, m, :], in0=n[:, m, :], in1=one_minus_u[:, m, :], op=ALU.mult)
+            nc.vector.tensor_tensor(out=blend[:, m, :], in0=blend[:, m, :], in1=u_h[:, m, :], op=ALU.add)
+            nc.sync.dma_start(out=out[0, P * m : P * (m + 1), :], in_=blend[:, m, :])

@@ -27,12 +27,12 @@ W_BUFS = 16
 FLOPS = 2 * 3 * GROUPS * P * PACK * H * L
 
 
-def load_scale_planes(nc, planes, scales):
-    by_offset = scales.bitcast(F32).rearrange("(c j) q n -> j q c n", j=CHUNK)
+def load_scale_planes(queue, word, planes, scales):
+    by_offset = scales.bitcast(word).rearrange("(c j) q n -> j q c n", j=CHUNK)
     for quadrant in range(4):
         for row in range(4):
-            nc.gpsimd.dma_start(
-                out=planes[32 * quadrant + row : 32 * quadrant + 4 * CHUNK : 4, :, :].bitcast(F32),
+            queue.dma_start(
+                out=planes[32 * quadrant + row : 32 * quadrant + 4 * CHUNK : 4, :, :].bitcast(word),
                 in_=by_offset[:, 4 * quadrant + row, :, :],
             )
 
@@ -77,9 +77,11 @@ def tile_gru_k_kernel(
         planes_h = keep.tile([P, CHUNKS, H], U8, align_bytes=64)
         identity = keep.tile([P, P], F32)
         make_identity(nc, identity[:])
-        for planes, scales in ((planes_r, w_r_scales), (planes_u, w_u_scales), (planes_h, w_h_scales)):
+        for planes in (planes_r, planes_u, planes_h):
             nc.vector.memset(planes[:].bitcast(I32), 0)
-            load_scale_planes(nc, planes, scales)
+        load_scale_planes(nc.sync, I32, planes_r, w_r_scales)
+        load_scale_planes(nc.gpsimd, F32, planes_u, w_u_scales)
+        load_scale_planes(nc.gpsimd, F32, planes_h, w_h_scales)
 
         h_by_k = keep.tile([P, PACK, L], BF16)
         h_by_tile = keep.tile([P, M_TILES, L], BF16)

@@ -19,41 +19,51 @@ H = 512
 X_GROUPS = 31
 GROUPS = X_GROUPS + 1
 HR_SLOT = GROUPS
-CHUNK = 4
-CHUNKS = GROUPS // CHUNK
+SHARE = 4
+LOAD = 8
 M_TILES = H // P
-W_BUFS = 16
+W_BUFS = 8
 
 FLOPS = 2 * 3 * GROUPS * P * PACK * H * L
 
 
-def load_scale_planes(queue, word, planes, scales):
-    by_offset = scales.bitcast(word).rearrange("(c j) q n -> j q c n", j=CHUNK)
+def cut_into_loads(tapered):
+    loads = []
+    first = 0
+    while first < GROUPS:
+        size = min(LOAD, max(1, (GROUPS - first) // 2)) if tapered else LOAD
+        loads.append((first, size))
+        first += size
+    return loads
+
+
+def load_scale_planes(nc, planes, scales):
+    by_offset = scales.bitcast(F32).rearrange("(c j) q n -> j q c n", j=SHARE)
     for quadrant in range(4):
         for row in range(4):
-            queue.dma_start(
-                out=planes[32 * quadrant + row : 32 * quadrant + 4 * CHUNK : 4, :, :].bitcast(word),
+            nc.gpsimd.dma_start(
+                out=planes[32 * quadrant + row : 32 * quadrant + 4 * SHARE : 4, :, :].bitcast(F32),
                 in_=by_offset[:, 4 * quadrant + row, :, :],
             )
 
 
-def load_words(nc, pool, words, c):
-    w = pool.tile([P, CHUNK, H], I32, tag="w", align_bytes=64)
-    rows = words[CHUNK * c : CHUNK * (c + 1)].rearrange("g p n t -> p g (n t)")
-    nc.sync.dma_start(out=w[:], in_=rows.bitcast(I32))
+def load_words(nc, pool, words, first, size):
+    w = pool.tile([P, LOAD, H], I32, tag="w", align_bytes=64)
+    rows = words[first : first + size].rearrange("g p n t -> p g (n t)")
+    nc.sync.dma_start(out=w[:, :size, :], in_=rows.bitcast(I32))
     return w
 
 
-def channel_major_passes(nc, acc, w, planes, c, codes, code_planes, last_slot):
+def channel_major_passes(nc, acc, w, first, size, planes, codes, code_planes, last_slot):
     for m in range(M_TILES):
         cols = slice(P * m, P * (m + 1))
-        for j in range(CHUNK):
-            g = CHUNK * c + j
+        for i in range(size):
+            g = first + i
             slot = g if g < GROUPS - 1 else last_slot
             nc.tensor.matmul_mx(
                 out=acc[m][:],
-                lhsT=w[:, j, cols].bitcast(FP8X4),
-                lhsT_scale=planes[4 * j : P, c, cols],
+                lhsT=w[:, i, cols].bitcast(FP8X4),
+                lhsT_scale=planes[4 * (g % SHARE) : P, g // SHARE, cols],
                 rhs=codes[:, slot, :].bitcast(FP8X4),
                 rhs_scale=code_planes[:, slot, :],
                 start=(g == 0),
@@ -68,63 +78,66 @@ def tile_gru_k_kernel(
     with ExitStack() as ctx:
         ctx.enter_context(tc.manual_schedule())
         keep = ctx.enter_context(tc.tile_pool(name="keep", bufs=1))
-        stage = ctx.enter_context(tc.tile_pool(name="stage", bufs=3))
+        stage = ctx.enter_context(tc.tile_pool(name="stage", bufs=2))
         stream = ctx.enter_context(tc.tile_pool(name="stream", bufs=W_BUFS))
         psum = ctx.enter_context(tc.psum_pool(name="psum", bufs=1))
 
-        planes_r = keep.tile([P, CHUNKS, H], U8, align_bytes=64)
-        planes_u = keep.tile([P, CHUNKS, H], U8, align_bytes=64)
-        planes_h = keep.tile([P, CHUNKS, H], U8, align_bytes=64)
+        planes_r = keep.tile([P, GROUPS // SHARE, H], U8, align_bytes=64)
+        planes_u = keep.tile([P, GROUPS // SHARE, H], U8, align_bytes=64)
+        planes_h = keep.tile([P, GROUPS // SHARE, H], U8, align_bytes=64)
         identity = keep.tile([P, P], F32)
         make_identity(nc, identity[:])
-        for planes in (planes_r, planes_u, planes_h):
+        for planes, scales in ((planes_r, w_r_scales), (planes_u, w_u_scales), (planes_h, w_h_scales)):
             nc.vector.memset(planes[:].bitcast(I32), 0)
-        load_scale_planes(nc.sync, I32, planes_r, w_r_scales)
-        load_scale_planes(nc.gpsimd, F32, planes_u, w_u_scales)
-        load_scale_planes(nc.gpsimd, F32, planes_h, w_h_scales)
+            load_scale_planes(nc, planes, scales)
 
         h_by_k = keep.tile([P, PACK, L], BF16)
         h_by_tile = keep.tile([P, M_TILES, L], BF16)
         nc.scalar.dma_start(out=h_by_k[:], in_=h[0].rearrange("(p t) l -> p t l", t=PACK))
         nc.scalar.dma_start(out=h_by_tile[:], in_=h[0].rearrange("(m p) l -> p m l", p=P))
         bias_r = keep.tile([P, PACK], BF16)
-        bias_u = keep.tile([P, M_TILES], BF16)
-        bias_h = keep.tile([P, M_TILES], BF16)
-        with nc.allow_non_contiguous_dma(reason="three biases of 512 values, one value a piece"):
-            nc.scalar.dma_start(out=bias_r[:], in_=b_r.rearrange("(p t) -> p t", t=PACK))
-            nc.scalar.dma_start(out=bias_u[:], in_=b_u.rearrange("(m p) -> p m", p=P))
-            nc.scalar.dma_start(out=bias_h[:], in_=b_h.rearrange("(m p) -> p m", p=P))
+        nc.scalar.dma_start(out=bias_r[:], in_=b_r.rearrange("(p t) -> p t", t=PACK))
+        bias_rows_bf16 = keep.tile([P, P], BF16)
+        nc.vector.memset(bias_rows_bf16[:], 0.0)
+        nc.scalar.dma_start(out=bias_rows_bf16[0:M_TILES, :], in_=b_u.rearrange("(m p) -> m p", p=P))
+        nc.scalar.dma_start(out=bias_rows_bf16[M_TILES : 2 * M_TILES, :], in_=b_h.rearrange("(m p) -> m p", p=P))
+        bias_rows = keep.tile([P, P], F32)
+        nc.vector.tensor_copy(out=bias_rows[:], in_=bias_rows_bf16[:])
+        bias_turned = psum.tile([P, P], F32, tag="bank1")
+        nc.tensor.transpose(bias_turned[:], bias_rows[:], identity[:])
+        bias_u_h = keep.tile([P, 2 * M_TILES], F32)
+        nc.vector.tensor_copy(out=bias_u_h[:], in_=bias_turned[:, 0 : 2 * M_TILES])
 
         codes = keep.tile([P, GROUPS + 1, L], U32, align_bytes=64)
         code_planes = keep.tile([P, GROUPS + 1, L], U8, align_bytes=64)
         x_by_k = x[0].rearrange("(g p t) l -> p g t l", p=P, t=PACK)
 
         acc_r = psum.tile([P, H], F32, tag="bank0")
-        for c in range(CHUNKS):
-            x_groups = min(CHUNK, X_GROUPS - CHUNK * c)
-            raw = stage.tile([P, CHUNK, PACK, L], BF16)
-            nc.sync.dma_start(out=raw[:, :x_groups], in_=x_by_k[:, CHUNK * c : CHUNK * c + x_groups])
-            w = load_words(nc, stream, w_r_words, c)
-            grouped = stage.tile([P, CHUNK, L, PACK], BF16, align_bytes=64)
+        for first, size in cut_into_loads(False):
+            x_groups = min(size, X_GROUPS - first)
+            raw = stage.tile([P, LOAD, PACK, L], BF16)
+            nc.sync.dma_start(out=raw[:, :x_groups], in_=x_by_k[:, first : first + x_groups])
+            w = load_words(nc, stream, w_r_words, first, size)
+            grouped = stage.tile([P, LOAD, L, PACK], BF16, align_bytes=64)
             nc.vector.tensor_copy(
                 out=grouped[:, :x_groups], in_=raw[:, :x_groups].rearrange("p g t l -> p g l t")
             )
-            if x_groups < CHUNK:
-                nc.vector.tensor_copy(out=grouped[:, CHUNK - 1], in_=h_by_k[:].rearrange("p t l -> p l t"))
-            slots = slice(CHUNK * c, CHUNK * (c + 1))
+            if x_groups < size:
+                nc.vector.tensor_copy(out=grouped[:, size - 1], in_=h_by_k[:].rearrange("p t l -> p l t"))
+            slots = slice(first, first + size)
             nc.vector.quantize_mx(
                 out=codes[:, slots, :].rearrange("p g l -> p (g l)").bitcast(FP8X4),
                 scales=code_planes[:, slots, :].rearrange("p g l -> p (g l)"),
                 in_=grouped[:].rearrange("p g l t -> p (g l t)"),
             )
-            for j in range(CHUNK):
-                g = CHUNK * c + j
+            for i in range(size):
+                g = first + i
                 nc.tensor.matmul_mx(
                     out=acc_r[:],
                     lhsT=codes[:, g, :].bitcast(FP8X4),
                     lhsT_scale=code_planes[:, g, :],
-                    rhs=w[:, j, :].bitcast(FP8X4),
-                    rhs_scale=planes_r[4 * j : P, c, :],
+                    rhs=w[:, i, :].bitcast(FP8X4),
+                    rhs_scale=planes_r[4 * (g % SHARE) : P, g // SHARE, :],
                     start=(g == 0),
                     stop=(g == GROUPS - 1),
                 )
@@ -151,12 +164,12 @@ def tile_gru_k_kernel(
         )
 
         acc_u = [psum.tile([P, L], F32, name="acc_u%d" % m, tag="bank%d" % (4 + m)) for m in range(M_TILES)]
-        for c in range(CHUNKS):
-            w = load_words(nc, stream, w_u_words, c)
-            channel_major_passes(nc, acc_u, w, planes_u, c, codes, code_planes, GROUPS - 1)
+        for first, size in cut_into_loads(False):
+            w = load_words(nc, stream, w_u_words, first, size)
+            channel_major_passes(nc, acc_u, w, first, size, planes_u, codes, code_planes, GROUPS - 1)
         u = keep.tile([P, M_TILES, L], F32)
         for m in range(M_TILES):
-            nc.scalar.activation(out=u[:, m, :], in_=acc_u[m][:], func=ACT.Sigmoid, bias=bias_u[:, m : m + 1])
+            nc.scalar.activation(out=u[:, m, :], in_=acc_u[m][:], func=ACT.Sigmoid, bias=bias_u_h[:, m : m + 1])
         one_minus_u = keep.tile([P, M_TILES, L], F32)
         nc.vector.tensor_scalar(
             out=one_minus_u[:], in0=u[:], scalar1=-1.0, scalar2=1.0, op0=ALU.mult, op1=ALU.add
@@ -165,13 +178,14 @@ def tile_gru_k_kernel(
         nc.vector.tensor_tensor(out=u_h[:], in0=u[:], in1=h_by_tile[:], op=ALU.mult)
 
         acc_n = [psum.tile([P, L], F32, name="acc_n%d" % m, tag="bank%d" % m) for m in range(M_TILES)]
-        for c in range(CHUNKS):
-            w = load_words(nc, stream, w_h_words, c)
-            channel_major_passes(nc, acc_n, w, planes_h, c, codes, code_planes, HR_SLOT)
+        for first, size in cut_into_loads(True):
+            w = load_words(nc, stream, w_h_words, first, size)
+            channel_major_passes(nc, acc_n, w, first, size, planes_h, codes, code_planes, HR_SLOT)
         n = keep.tile([P, M_TILES, L], F32)
         blend = keep.tile([P, M_TILES, L], F32)
         for m in range(M_TILES):
-            nc.scalar.activation(out=n[:, m, :], in_=acc_n[m][:], func=ACT.Tanh, bias=bias_h[:, m : m + 1])
+            bias_h = bias_u_h[:, M_TILES + m : M_TILES + m + 1]
+            nc.scalar.activation(out=n[:, m, :], in_=acc_n[m][:], func=ACT.Tanh, bias=bias_h)
             nc.vector.tensor_tensor(out=blend[:, m, :], in0=n[:, m, :], in1=one_minus_u[:, m, :], op=ALU.mult)
             nc.vector.tensor_tensor(out=blend[:, m, :], in0=blend[:, m, :], in1=u_h[:, m, :], op=ALU.add)
             nc.sync.dma_start(out=out[0, P * m : P * (m + 1), :], in_=blend[:, m, :])

@@ -37,11 +37,11 @@ def cut_into_loads(tapered):
     return loads
 
 
-def load_scale_planes(nc, planes, scales):
+def load_scale_planes(queue, planes, scales, quadrants):
     by_offset = scales.bitcast(F32).rearrange("(c j) q n -> j q c n", j=SHARE)
-    for quadrant in range(4):
+    for quadrant in quadrants:
         for row in range(4):
-            nc.gpsimd.dma_start(
+            queue.dma_start(
                 out=planes[32 * quadrant + row : 32 * quadrant + 4 * SHARE : 4, :, :].bitcast(F32),
                 in_=by_offset[:, 4 * quadrant + row, :, :],
             )
@@ -87,9 +87,10 @@ def tile_gru_k_kernel(
         planes_h = keep.tile([P, GROUPS // SHARE, H], U8, align_bytes=64)
         identity = keep.tile([P, P], F32)
         make_identity(nc, identity[:])
-        for planes, scales in ((planes_r, w_r_scales), (planes_u, w_u_scales), (planes_h, w_h_scales)):
+        weights = ((planes_r, w_r_scales), (planes_u, w_u_scales), (planes_h, w_h_scales))
+        for planes, scales in weights:
             nc.vector.memset(planes[:].bitcast(I32), 0)
-            load_scale_planes(nc, planes, scales)
+            load_scale_planes(nc.gpsimd, planes, scales, (2, 3))
 
         h_by_k = keep.tile([P, PACK, L], BF16)
         h_by_tile = keep.tile([P, M_TILES, L], BF16)
@@ -118,6 +119,9 @@ def tile_gru_k_kernel(
             raw = stage.tile([P, LOAD, PACK, L], BF16)
             nc.sync.dma_start(out=raw[:, :x_groups], in_=x_by_k[:, first : first + x_groups])
             w = load_words(nc, stream, w_r_words, first, size)
+            if first // LOAD < len(weights):
+                planes, scales = weights[first // LOAD]
+                load_scale_planes(nc.scalar, planes, scales, (0, 1))
             grouped = stage.tile([P, LOAD, L, PACK], BF16, align_bytes=64)
             nc.vector.tensor_copy(
                 out=grouped[:, :x_groups], in_=raw[:, :x_groups].rearrange("p g t l -> p g l t")
@@ -183,9 +187,14 @@ def tile_gru_k_kernel(
             channel_major_passes(nc, acc_n, w, first, size, planes_h, codes, code_planes, HR_SLOT)
         n = keep.tile([P, M_TILES, L], F32)
         blend = keep.tile([P, M_TILES, L], F32)
+        scaled = keep.tile([P, M_TILES, L], F32)
         for m in range(M_TILES):
             bias_h = bias_u_h[:, M_TILES + m : M_TILES + m + 1]
             nc.scalar.activation(out=n[:, m, :], in_=acc_n[m][:], func=ACT.Tanh, bias=bias_h)
-            nc.vector.tensor_tensor(out=blend[:, m, :], in0=n[:, m, :], in1=one_minus_u[:, m, :], op=ALU.mult)
-            nc.vector.tensor_tensor(out=blend[:, m, :], in0=blend[:, m, :], in1=u_h[:, m, :], op=ALU.add)
-            nc.sync.dma_start(out=out[0, P * m : P * (m + 1), :], in_=blend[:, m, :])
+        for pair in ((0, 1), (2, 3)):
+            for m in pair:
+                nc.vector.tensor_tensor(out=scaled[:, m, :], in0=n[:, m, :], in1=one_minus_u[:, m, :], op=ALU.mult)
+            for m in pair:
+                nc.vector.tensor_tensor(out=blend[:, m, :], in0=scaled[:, m, :], in1=u_h[:, m, :], op=ALU.add)
+                queue = nc.sync if m % 2 == 0 else nc.scalar
+                queue.dma_start(out=out[0, P * m : P * (m + 1), :], in_=blend[:, m, :])

from contextlib import ExitStack

import concourse.mybir as mybir
from concourse.masks import make_identity

F32 = mybir.dt.float32
BF16 = mybir.dt.bfloat16
I32 = mybir.dt.int32
U32 = mybir.dt.uint32
U8 = mybir.dt.uint8
FP8X4 = mybir.dt.float8_e4m3fn_x4
ACT = mybir.ActivationFunctionType
ALU = mybir.AluOpType

P = 128
PACK = 4
L = 128
H = 512
X_GROUPS = 31
GROUPS = X_GROUPS + 1
HR_SLOT = GROUPS
SHARE = 4
LOAD = 8
M_TILES = H // P
W_BUFS = 8

FLOPS = 2 * 3 * GROUPS * P * PACK * H * L


def cut_into_loads(tapered):
    loads = []
    first = 0
    while first < GROUPS:
        size = min(LOAD, max(1, (GROUPS - first) // 2)) if tapered else LOAD
        loads.append((first, size))
        first += size
    return loads


def load_scale_planes(queue, planes, scales, quadrants):
    by_offset = scales.bitcast(F32).rearrange("(c j) q n -> j q c n", j=SHARE)
    for quadrant in quadrants:
        for row in range(4):
            queue.dma_start(
                out=planes[32 * quadrant + row : 32 * quadrant + 4 * SHARE : 4, :, :].bitcast(F32),
                in_=by_offset[:, 4 * quadrant + row, :, :],
            )


def load_words(nc, pool, words, first, size):
    w = pool.tile([P, LOAD, H], I32, tag="w", align_bytes=64)
    rows = words[first : first + size].rearrange("g p n t -> p g (n t)")
    nc.sync.dma_start(out=w[:, :size, :], in_=rows.bitcast(I32))
    return w


def channel_major_passes(nc, acc, w, first, size, planes, codes, code_planes, last_slot):
    for m in range(M_TILES):
        cols = slice(P * m, P * (m + 1))
        for i in range(size):
            g = first + i
            slot = g if g < GROUPS - 1 else last_slot
            nc.tensor.matmul_mx(
                out=acc[m][:],
                lhsT=w[:, i, cols].bitcast(FP8X4),
                lhsT_scale=planes[4 * (g % SHARE) : P, g // SHARE, cols],
                rhs=codes[:, slot, :].bitcast(FP8X4),
                rhs_scale=code_planes[:, slot, :],
                start=(g == 0),
                stop=(g == GROUPS - 1),
            )


def tile_gru_k_kernel(
    tc, x, h, w_r_words, w_r_scales, b_r, w_u_words, w_u_scales, b_u, w_h_words, w_h_scales, b_h, out
):
    nc = tc.nc
    with ExitStack() as ctx:
        ctx.enter_context(tc.manual_schedule())
        keep = ctx.enter_context(tc.tile_pool(name="keep", bufs=1))
        stage = ctx.enter_context(tc.tile_pool(name="stage", bufs=2))
        stream = ctx.enter_context(tc.tile_pool(name="stream", bufs=W_BUFS))
        psum = ctx.enter_context(tc.psum_pool(name="psum", bufs=1))

        planes_r = keep.tile([P, GROUPS // SHARE, H], U8, align_bytes=64)
        planes_u = keep.tile([P, GROUPS // SHARE, H], U8, align_bytes=64)
        planes_h = keep.tile([P, GROUPS // SHARE, H], U8, align_bytes=64)
        identity = keep.tile([P, P], F32)
        make_identity(nc, identity[:])
        weights = ((planes_r, w_r_scales), (planes_u, w_u_scales), (planes_h, w_h_scales))
        for planes, scales in weights:
            nc.vector.memset(planes[:].bitcast(I32), 0)
            load_scale_planes(nc.gpsimd, planes, scales, (2, 3))

        h_by_k = keep.tile([P, PACK, L], BF16)
        h_by_tile = keep.tile([P, M_TILES, L], BF16)
        nc.scalar.dma_start(out=h_by_k[:], in_=h[0].rearrange("(p t) l -> p t l", t=PACK))
        nc.scalar.dma_start(out=h_by_tile[:], in_=h[0].rearrange("(m p) l -> p m l", p=P))
        bias_r = keep.tile([P, PACK], BF16)
        nc.scalar.dma_start(out=bias_r[:], in_=b_r.rearrange("(p t) -> p t", t=PACK))
        bias_rows_bf16 = keep.tile([P, P], BF16)
        nc.vector.memset(bias_rows_bf16[:], 0.0)
        nc.scalar.dma_start(out=bias_rows_bf16[0:M_TILES, :], in_=b_u.rearrange("(m p) -> m p", p=P))
        nc.scalar.dma_start(out=bias_rows_bf16[M_TILES : 2 * M_TILES, :], in_=b_h.rearrange("(m p) -> m p", p=P))
        bias_rows = keep.tile([P, P], F32)
        nc.vector.tensor_copy(out=bias_rows[:], in_=bias_rows_bf16[:])
        bias_turned = psum.tile([P, P], F32, tag="bank1")
        nc.tensor.transpose(bias_turned[:], bias_rows[:], identity[:])
        bias_u_h = keep.tile([P, 2 * M_TILES], F32)
        nc.vector.tensor_copy(out=bias_u_h[:], in_=bias_turned[:, 0 : 2 * M_TILES])

        codes = keep.tile([P, GROUPS + 1, L], U32, align_bytes=64)
        code_planes = keep.tile([P, GROUPS + 1, L], U8, align_bytes=64)
        x_by_k = x[0].rearrange("(g p t) l -> p g t l", p=P, t=PACK)

        acc_r = psum.tile([P, H], F32, tag="bank0")
        for first, size in cut_into_loads(False):
            x_groups = min(size, X_GROUPS - first)
            raw = stage.tile([P, LOAD, PACK, L], BF16)
            nc.sync.dma_start(out=raw[:, :x_groups], in_=x_by_k[:, first : first + x_groups])
            w = load_words(nc, stream, w_r_words, first, size)
            if first // LOAD < len(weights):
                planes, scales = weights[first // LOAD]
                load_scale_planes(nc.scalar, planes, scales, (0, 1))
            grouped = stage.tile([P, LOAD, L, PACK], BF16, align_bytes=64)
            nc.vector.tensor_copy(
                out=grouped[:, :x_groups], in_=raw[:, :x_groups].rearrange("p g t l -> p g l t")
            )
            if x_groups < size:
                nc.vector.tensor_copy(out=grouped[:, size - 1], in_=h_by_k[:].rearrange("p t l -> p l t"))
            slots = slice(first, first + size)
            nc.vector.quantize_mx(
                out=codes[:, slots, :].rearrange("p g l -> p (g l)").bitcast(FP8X4),
                scales=code_planes[:, slots, :].rearrange("p g l -> p (g l)"),
                in_=grouped[:].rearrange("p g l t -> p (g l t)"),
            )
            for i in range(size):
                g = first + i
                nc.tensor.matmul_mx(
                    out=acc_r[:],
                    lhsT=codes[:, g, :].bitcast(FP8X4),
                    lhsT_scale=code_planes[:, g, :],
                    rhs=w[:, i, :].bitcast(FP8X4),
                    rhs_scale=planes_r[4 * (g % SHARE) : P, g // SHARE, :],
                    start=(g == 0),
                    stop=(g == GROUPS - 1),
                )

        r_pre_t = keep.tile([P, PACK, P], F32)
        nc.vector.tensor_copy(out=r_pre_t[:], in_=acc_r[:].rearrange("l (p t) -> l t p", t=PACK))
        r_pre = psum.tile([P, PACK, L], F32, tag="bank1")
        for t in range(PACK):
            nc.tensor.transpose(r_pre[:, t, :], r_pre_t[:, t, :], identity[:])
        r = keep.tile([P, PACK, L], F32)
        for t in range(PACK):
            nc.scalar.activation(out=r[:, t, :], in_=r_pre[:, t, :], func=ACT.Sigmoid, bias=bias_r[:, t : t + 1])
        hr_grouped = keep.tile([P, L, PACK], BF16, align_bytes=64)
        nc.vector.tensor_tensor(
            out=hr_grouped[:],
            in0=h_by_k[:].rearrange("p t l -> p l t"),
            in1=r[:].rearrange("p t l -> p l t"),
            op=ALU.mult,
        )
        nc.vector.quantize_mx(
            out=codes[:, HR_SLOT, :].bitcast(FP8X4),
            scales=code_planes[:, HR_SLOT, :],
            in_=hr_grouped[:].rearrange("p l t -> p (l t)"),
        )

        acc_u = [psum.tile([P, L], F32, name="acc_u%d" % m, tag="bank%d" % (4 + m)) for m in range(M_TILES)]
        for first, size in cut_into_loads(False):
            w = load_words(nc, stream, w_u_words, first, size)
            channel_major_passes(nc, acc_u, w, first, size, planes_u, codes, code_planes, GROUPS - 1)
        u = keep.tile([P, M_TILES, L], F32)
        for m in range(M_TILES):
            nc.scalar.activation(out=u[:, m, :], in_=acc_u[m][:], func=ACT.Sigmoid, bias=bias_u_h[:, m : m + 1])
        one_minus_u = keep.tile([P, M_TILES, L], F32)
        nc.vector.tensor_scalar(
            out=one_minus_u[:], in0=u[:], scalar1=-1.0, scalar2=1.0, op0=ALU.mult, op1=ALU.add
        )
        u_h = keep.tile([P, M_TILES, L], F32)
        nc.vector.tensor_tensor(out=u_h[:], in0=u[:], in1=h_by_tile[:], op=ALU.mult)

        acc_n = [psum.tile([P, L], F32, name="acc_n%d" % m, tag="bank%d" % m) for m in range(M_TILES)]
        for first, size in cut_into_loads(True):
            w = load_words(nc, stream, w_h_words, first, size)
            channel_major_passes(nc, acc_n, w, first, size, planes_h, codes, code_planes, HR_SLOT)
        n = keep.tile([P, M_TILES, L], F32)
        blend = keep.tile([P, M_TILES, L], F32)
        scaled = keep.tile([P, M_TILES, L], F32)
        for m in range(M_TILES):
            bias_h = bias_u_h[:, M_TILES + m : M_TILES + m + 1]
            nc.scalar.activation(out=n[:, m, :], in_=acc_n[m][:], func=ACT.Tanh, bias=bias_h)
        for pair in ((0, 1), (2, 3)):
            for m in pair:
                nc.vector.tensor_tensor(out=scaled[:, m, :], in0=n[:, m, :], in1=one_minus_u[:, m, :], op=ALU.mult)
            for m in pair:
                nc.vector.tensor_tensor(out=blend[:, m, :], in0=scaled[:, m, :], in1=u_h[:, m, :], op=ALU.add)
                queue = nc.sync if m % 2 == 0 else nc.scalar
                queue.dma_start(out=out[0, P * m : P * (m + 1), :], in_=blend[:, m, :])
